import numpy as np
import ml_dtypes


def mxq(x, axis, fmt="e4m3"):
    dtype, down = {"e4m3": (ml_dtypes.float8_e4m3fn, 7), "e5m2": (ml_dtypes.float8_e5m2, 14)}[fmt]
    v = np.moveaxis(np.asarray(x, np.float32).astype(ml_dtypes.bfloat16).astype(np.float64), axis, -1)
    blocks = v.reshape(v.shape[:-1] + (-1, 32))
    amax = np.abs(blocks).max(-1, keepdims=True)
    byte = np.maximum(np.where(amax > 0, np.frexp(amax)[1] - 1 + 127, 0) - down, 1)
    scale = np.exp2(byte - 127.0)
    codes = (blocks / scale).astype(np.float32).astype(dtype).astype(np.float64)
    return np.moveaxis((codes * scale).reshape(v.shape), -1, axis)


BF16 = ml_dtypes.bfloat16


def bf(x):
    return np.asarray(x, np.float32).astype(BF16)


def f64(x):
    return np.asarray(x).astype(np.float64)


B, C, H, W, G = 2, 256, 48, 32, 16
N = B * H * W


def setup_inputs():
    a = 2.0 / C ** 0.25
    centres = np.random.standard_normal((G, C)) * a
    f = centres[np.random.randint(0, G, N)] + np.random.standard_normal((N, C)) * a
    return {"hidden_states": bf(np.ascontiguousarray(f.reshape(B, H, W, C).transpose(0, 3, 1, 2)))}


def reference(hidden_states):
    lam = np.sqrt(C)
    f = f64(hidden_states).transpose(0, 2, 3, 1).reshape(N, C)
    scores = f @ f.T / lam
    e = np.exp(scores - scores.max(-1, keepdims=True))
    attn = e / e.sum(-1, keepdims=True)
    out = mxq(attn, 1, "e4m3") @ mxq(f, 0, "e4m3")
    return np.ascontiguousarray(out.reshape(B, H, W, C).transpose(0, 3, 1, 2))

@@ -1,0 +1,252 @@
+from contextlib import ExitStack
+
+import concourse.mybir as mybir
+from concourse.masks import make_identity
+
+F32 = mybir.dt.float32
+BF16 = mybir.dt.bfloat16
+U32 = mybir.dt.uint32
+U8 = mybir.dt.uint8
+FP8X4 = mybir.dt.float8_e4m3fn_x4
+AF = mybir.ActivationFunctionType
+ALU = mybir.AluOpType
+AX = mybir.AxisListType
+
+P = 128
+C = 256
+NTOK = 3072
+NB = NTOK // P
+NG = NTOK // 512
+HALF = 1536
+FLOPS = 2 * 2 * NTOK * NTOK * C
+INV = 1.0 / 16.0
+
+
+def tile_trainingfreeselfattention_kernel(tc, hidden_states, out):
+    nc = tc.nc
+    x = hidden_states.rearrange("b c h w -> b c (h w)")
+    y = out.rearrange("b c h w -> b c (h w)")
+
+    with ExitStack() as ctx:
+        keep = ctx.enter_context(tc.tile_pool(name="keep", bufs=1))
+        small = ctx.enter_context(tc.tile_pool(name="small", bufs=4))
+        big = ctx.enter_context(tc.tile_pool(name="big", bufs=3))
+        stage = ctx.enter_context(tc.tile_pool(name="stage", bufs=3))
+        ps_s = ctx.enter_context(tc.psum_pool(name="ps_s", bufs=6))
+        ps_a = ctx.enter_context(tc.psum_pool(name="ps_a", bufs=2))
+        ctx.enter_context(tc.manual_schedule())
+
+        f_t = keep.tile([P, 2, NTOK], BF16, name="f_t")
+        f_p = keep.tile([P, 2, NTOK], BF16, name="f_p")
+        ident = keep.tile([P, P], F32, name="ident")
+        f_codes = keep.tile([P, NG * C], U32, name="f_codes", align_bytes=64)
+        f_scales = keep.tile([P, NG * C], U8, name="f_scales", align_bytes=64)
+        o_sb = keep.tile([P, 2, NTOK], F32, name="o_sb")
+        warm_in = keep.tile([P, 1], F32, name="warm_in")
+        warm_out = keep.tile([P, 1], F32, name="warm_out")
+
+        for b in range(2):
+            for h in range(2):
+                nc.sync.dma_start(
+                    out=f_t[:, h, HALF * b : HALF * (b + 1)],
+                    in_=x[b, P * h : P * (h + 1), :],
+                )
+        nc.vector.memset(warm_in[:], 0.0)
+        nc.scalar.activation(out=warm_out[:], in_=warm_in[:], func=AF.Exp)
+        make_identity(nc, ident[:])
+
+        for g in range(NG):
+            for h in range(2):
+                src = f_t[:, h, 512 * g : 512 * (g + 1)].bitcast(F32).rearrange(
+                    "p (q u) -> p u q", u=2
+                )
+                dst = f_p[:, h, 512 * g : 512 * (g + 1)].bitcast(F32).rearrange(
+                    "p (u q) -> p u q", u=2
+                )
+                if h == 0:
+                    nc.vector.tensor_copy(out=dst, in_=src)
+                else:
+                    nc.scalar.copy(out=dst, in_=src)
+
+        st = {}
+
+        def transp_a(i, w):
+            if w % 4 == 0:
+                st[("t", i, w // 4)] = ps_a.tile([P, 2, 2, P], F32, name="t", tag="aux")
+            nc.tensor.transpose(
+                st[("t", i, w // 4)][:, (w // 2) % 2, w % 2, :],
+                st[("a", i)][:].bitcast(F32)[:, P * w : P * (w + 1)],
+                ident[:],
+            )
+
+        def transp_f(i, w):
+            g = 3 * (i + 2) + w // 4
+            if w % 4 == 0:
+                st[("t", i, w // 4)] = ps_a.tile([P, 2, C], F32, name="tf", tag="aux")
+            u = (w // 2) % 2
+            h = w % 2
+            c0 = 256 * g + P * u
+            nc.tensor.transpose(
+                st[("t", i, w // 4)][:, u, P * h : P * (h + 1)],
+                f_p[:, h, :].bitcast(F32)[:, c0 : c0 + P],
+                ident[:],
+            )
+
+        def transp(i, w):
+            if -2 <= i < 0:
+                transp_f(i, w)
+            elif 0 <= i < NB:
+                transp_a(i, w)
+
+        def score(i, g, weave):
+            s = ps_s.tile([P, 512], F32, name="s", tag="s")
+            st[("s", i, g)] = s
+            for h in range(2):
+                nc.tensor.matmul(
+                    s[:],
+                    lhsT=f_t[:, h, P * i : P * (i + 1)],
+                    rhs=f_p[:, h, 512 * g : 512 * (g + 1)],
+                    start=(h == 0),
+                    stop=(h == 1),
+                )
+                if weave is not None:
+                    transp(weave[0], weave[1] + h)
+            if g == 0:
+                st[("m6", i)] = small.tile([P, NG], F32, name="m6", tag="m6")
+            nc.vector.tensor_reduce(
+                out=st[("m6", i)][:, g : g + 1], in_=s[:], axis=AX.X, op=ALU.max
+            )
+
+        def bias(i):
+            top = small.tile([P, 1], F32, name="top", tag="top")
+            nb = small.tile([P, 1], F32, name="nb", tag="nb")
+            nc.vector.tensor_reduce(out=top[:], in_=st[("m6", i)][:], axis=AX.X, op=ALU.max)
+            nc.vector.tensor_scalar(
+                out=nb[:], in0=top[:], scalar1=-INV, scalar2=None, op0=ALU.mult
+            )
+            st[("nb", i)] = nb
+
+        def expo(i, g):
+            if g == 0:
+                st[("e", i)] = big.tile([P, NTOK], F32, name="e", tag="e")
+                st[("s6", i)] = small.tile([P, NG], F32, name="s6", tag="s6")
+            nc.scalar.activation(
+                out=st[("e", i)][:, 512 * g : 512 * (g + 1)],
+                in_=st[("s", i, g)][:],
+                func=AF.Exp,
+                bias=st[("nb", i)][:, 0:1],
+                scale=INV,
+                accum_out=st[("s6", i)][:, g : g + 1],
+            )
+
+        def recip(i):
+            tot = small.tile([P, 1], F32, name="tot", tag="tot")
+            r = small.tile([P, 1], F32, name="r", tag="r")
+            nc.vector.tensor_reduce(out=tot[:], in_=st[("s6", i)][:], axis=AX.X, op=ALU.add)
+            nc.vector.reciprocal(out=r[:], in_=tot[:])
+            st[("r", i)] = r
+
+        def norm(i, k):
+            if k == 0:
+                st[("a", i)] = big.tile([P, NTOK], BF16, name="a", tag="a")
+            nc.gpsimd.tensor_scalar(
+                out=st[("a", i)][:, 1024 * k : 1024 * (k + 1)],
+                in0=st[("e", i)][:, 1024 * k : 1024 * (k + 1)],
+                scalar1=st[("r", i)][:, 0:1],
+                scalar2=0.0,
+                op0=ALU.mult,
+                op1=ALU.add,
+            )
+
+        def evac(i, k):
+            if not -2 <= i < NB:
+                return
+            if k == 0:
+                st[("g4", i)] = stage.tile([P, NTOK], BF16, name="g4", tag="g4", align_bytes=64)
+            dst32 = st[("g4", i)][:].bitcast(F32)[:, 512 * k : 512 * (k + 1)]
+            if i < 0:
+                nc.scalar.copy(
+                    out=dst32.rearrange("p (c u) -> p c u", u=2),
+                    in_=st[("t", i, k)][:].rearrange("p u c -> p c u"),
+                )
+            else:
+                nc.scalar.copy(
+                    out=dst32.rearrange("p (g n u) -> p g n u", g=2, u=2),
+                    in_=st[("t", i, k)][:].rearrange("p g u n -> p g n u"),
+                )
+
+        def quant(i, k):
+            if not -2 <= i < NB:
+                return
+            src = st[("g4", i)][:, 1024 * k : 1024 * (k + 1)]
+            if i < 0:
+                g = 3 * (i + 2) + k
+                nc.vector.quantize_mx(
+                    out=f_codes[:, C * g : C * (g + 1)].bitcast(FP8X4),
+                    scales=f_scales[:, C * g : C * (g + 1)],
+                    in_=src,
+                )
+                return
+            if k == 0:
+                st[("qc", i)] = stage.tile([P, NG * P], U32, name="qc", tag="qc", align_bytes=64)
+                st[("qs", i)] = stage.tile([P, NG * P], U8, name="qs", tag="qs", align_bytes=64)
+            nc.vector.quantize_mx(
+                out=st[("qc", i)][:, 256 * k : 256 * (k + 1)].bitcast(FP8X4),
+                scales=st[("qs", i)][:, 256 * k : 256 * (k + 1)],
+                in_=src,
+            )
+
+        def mx(i):
+            o_ps = ps_a.tile([P, 2, P], F32, name="o_ps", tag="aux")
+            for h in range(2):
+                for g in range(NG):
+                    w0 = C * g + P * h
+                    nc.tensor.matmul_mx(
+                        out=o_ps[:, h, :],
+                        lhsT=f_codes[:, w0 : w0 + P].bitcast(FP8X4),
+                        lhsT_scale=f_scales[:, w0 : w0 + P],
+                        rhs=st[("qc", i)][:, P * g : P * (g + 1)].bitcast(FP8X4),
+                        rhs_scale=st[("qs", i)][:, P * g : P * (g + 1)],
+                        start=(g == 0),
+                        stop=(g == NG - 1),
+                    )
+            nc.vector.tensor_copy(out=o_sb[:, :, P * i : P * (i + 1)], in_=o_ps[:])
+            if i % 4 == 3:
+                n0 = P * (i - 3)
+                b = n0 // HALF
+                for h in range(2):
+                    nc.sync.dma_start(
+                        out=y[b, P * h : P * (h + 1), n0 - HALF * b : n0 - HALF * b + 512],
+                        in_=o_sb[:, h, n0 : n0 + 512],
+                    )
+
+        for g in range(NG):
+            score(0, g, None)
+        bias(0)
+
+        for i in range(NB + 3):
+            if 0 <= i - 1 < NB:
+                for k in range(3):
+                    norm(i - 1, k)
+            for g in range(NG):
+                if i < NB:
+                    expo(i, g)
+                weave = (i - 2, 2 * (g - 1)) if 1 <= g <= 4 else None
+                if i + 1 < NB:
+                    score(i + 1, g, weave)
+                elif weave is not None:
+                    transp(weave[0], weave[1])
+                    transp(weave[0], weave[1] + 1)
+            if i + 1 < NB:
+                bias(i + 1)
+            evac(i - 2, 0)
+            evac(i - 2, 1)
+            for w in range(8, 12):
+                transp(i - 2, w)
+            evac(i - 2, 2)
+            for k in range(3):
+                quant(i - 2, k)
+            if i < NB:
+                recip(i)
+            if 0 <= i - 3 < NB:
+                mx(i - 3)

@@ -20,6 +20,7 @@ NG = NTOK // 512
 HALF = 1536
 FLOPS = 2 * 2 * NTOK * NTOK * C
 INV = 1.0 / 16.0
+STORE_AFTER = {3: 4, 7: 4, 11: 4, 15: 4, 19: 4, 22: 3, 23: 1}
 
 
 def tile_trainingfreeselfattention_kernel(tc, hidden_states, out):
@@ -30,10 +31,11 @@ def tile_trainingfreeselfattention_kernel(tc, hidden_states, out):
     with ExitStack() as ctx:
         keep = ctx.enter_context(tc.tile_pool(name="keep", bufs=1))
         small = ctx.enter_context(tc.tile_pool(name="small", bufs=4))
-        big = ctx.enter_context(tc.tile_pool(name="big", bufs=3))
+        big = ctx.enter_context(tc.tile_pool(name="big", bufs=4))
         stage = ctx.enter_context(tc.tile_pool(name="stage", bufs=3))
-        ps_s = ctx.enter_context(tc.psum_pool(name="ps_s", bufs=6))
-        ps_a = ctx.enter_context(tc.psum_pool(name="ps_a", bufs=2))
+        ps_s = ctx.enter_context(tc.psum_pool(name="ps_s", bufs=3))
+        ps_t = ctx.enter_context(tc.psum_pool(name="ps_t", bufs=3))
+        ps_o = ctx.enter_context(tc.psum_pool(name="ps_o", bufs=2))
         ctx.enter_context(tc.manual_schedule())
 
         f_t = keep.tile([P, 2, NTOK], BF16, name="f_t")
@@ -70,37 +72,35 @@ def tile_trainingfreeselfattention_kernel(tc, hidden_states, out):
 
         st = {}
 
-        def transp_a(i, w):
+        def transp(i, w):
+            if not -2 <= i < NB:
+                return
+            if i < 0:
+                g = 3 * (i + 2) + w // 4
+                if w % 4 == 0:
+                    st[("t", i, w // 4)] = ps_t.tile([P, 2, C], F32, name="tf", tag="t")
+                u = (w // 2) % 2
+                h = w % 2
+                c0 = 256 * g + P * u
+                nc.tensor.transpose(
+                    st[("t", i, w // 4)][:, u, P * h : P * (h + 1)],
+                    f_p[:, h, :].bitcast(F32)[:, c0 : c0 + P],
+                    ident[:],
+                )
+                return
             if w % 4 == 0:
-                st[("t", i, w // 4)] = ps_a.tile([P, 2, 2, P], F32, name="t", tag="aux")
+                st[("t", i, w // 4)] = ps_t.tile([P, 2, 2, P], F32, name="t", tag="t")
             nc.tensor.transpose(
                 st[("t", i, w // 4)][:, (w // 2) % 2, w % 2, :],
                 st[("a", i)][:].bitcast(F32)[:, P * w : P * (w + 1)],
                 ident[:],
             )
 
-        def transp_f(i, w):
-            g = 3 * (i + 2) + w // 4
-            if w % 4 == 0:
-                st[("t", i, w // 4)] = ps_a.tile([P, 2, C], F32, name="tf", tag="aux")
-            u = (w // 2) % 2
-            h = w % 2
-            c0 = 256 * g + P * u
-            nc.tensor.transpose(
-                st[("t", i, w // 4)][:, u, P * h : P * (h + 1)],
-                f_p[:, h, :].bitcast(F32)[:, c0 : c0 + P],
-                ident[:],
-            )
-
-        def transp(i, w):
-            if -2 <= i < 0:
-                transp_f(i, w)
-            elif 0 <= i < NB:
-                transp_a(i, w)
-
-        def score(i, g, weave):
+        def score(i, g, j):
+            if g == 0:
+                st[("e", i)] = big.tile([P, NTOK], F32, name="e", tag="e")
+                st[("m6", i)] = small.tile([P, NG], F32, name="m6", tag="m6")
             s = ps_s.tile([P, 512], F32, name="s", tag="s")
-            st[("s", i, g)] = s
             for h in range(2):
                 nc.tensor.matmul(
                     s[:],
@@ -109,33 +109,38 @@ def tile_trainingfreeselfattention_kernel(tc, hidden_states, out):
                     start=(h == 0),
                     stop=(h == 1),
                 )
-                if weave is not None:
-                    transp(weave[0], weave[1] + h)
-            if g == 0:
-                st[("m6", i)] = small.tile([P, NG], F32, name="m6", tag="m6")
-            nc.vector.tensor_reduce(
-                out=st[("m6", i)][:, g : g + 1], in_=s[:], axis=AX.X, op=ALU.max
+                m = 2 * g + h
+                if m < 10:
+                    transp(j, m)
+                elif m == 10:
+                    transp(j, 10)
+                    transp(j, 11)
+            nc.vector.tensor_scalar(
+                out=st[("e", i)][:, 512 * g : 512 * (g + 1)],
+                in0=s[:],
+                scalar1=INV,
+                scalar2=None,
+                op0=ALU.mult,
+                op1=ALU.max,
+                accum_out=st[("m6", i)][:, g : g + 1],
             )
 
         def bias(i):
-            top = small.tile([P, 1], F32, name="top", tag="top")
             nb = small.tile([P, 1], F32, name="nb", tag="nb")
-            nc.vector.tensor_reduce(out=top[:], in_=st[("m6", i)][:], axis=AX.X, op=ALU.max)
-            nc.vector.tensor_scalar(
-                out=nb[:], in0=top[:], scalar1=-INV, scalar2=None, op0=ALU.mult
+            nc.vector.tensor_reduce(
+                out=nb[:], in_=st[("m6", i)][:], axis=AX.X, op=ALU.max, negate=True
             )
             st[("nb", i)] = nb
 
         def expo(i, g):
             if g == 0:
-                st[("e", i)] = big.tile([P, NTOK], F32, name="e", tag="e")
                 st[("s6", i)] = small.tile([P, NG], F32, name="s6", tag="s6")
             nc.scalar.activation(
                 out=st[("e", i)][:, 512 * g : 512 * (g + 1)],
-                in_=st[("s", i, g)][:],
+                in_=st[("e", i)][:, 512 * g : 512 * (g + 1)],
                 func=AF.Exp,
                 bias=st[("nb", i)][:, 0:1],
-                scale=INV,
+                scale=1.0,
                 accum_out=st[("s6", i)][:, g : g + 1],
             )
 
@@ -149,14 +154,17 @@ def tile_trainingfreeselfattention_kernel(tc, hidden_states, out):
         def norm(i, k):
             if k == 0:
                 st[("a", i)] = big.tile([P, NTOK], BF16, name="a", tag="a")
-            nc.gpsimd.tensor_scalar(
-                out=st[("a", i)][:, 1024 * k : 1024 * (k + 1)],
-                in0=st[("e", i)][:, 1024 * k : 1024 * (k + 1)],
-                scalar1=st[("r", i)][:, 0:1],
-                scalar2=0.0,
-                op0=ALU.mult,
-                op1=ALU.add,
-            )
+            dst = st[("a", i)][:, 1024 * k : 1024 * (k + 1)]
+            src = st[("e", i)][:, 1024 * k : 1024 * (k + 1)]
+            r = st[("r", i)][:, 0:1]
+            if i == NB - 1 and k == 0:
+                nc.vector.tensor_scalar(out=dst, in0=src, scalar1=r, scalar2=None, op0=ALU.mult)
+            elif i == NB - 1 and k == 1:
+                nc.scalar.activation(out=dst, in_=src, func=AF.Copy, scale=r)
+            else:
+                nc.gpsimd.tensor_scalar(
+                    out=dst, in0=src, scalar1=r, scalar2=0.0, op0=ALU.mult, op1=ALU.add
+                )
 
         def evac(i, k):
             if not -2 <= i < NB:
@@ -197,7 +205,8 @@ def tile_trainingfreeselfattention_kernel(tc, hidden_states, out):
             )
 
         def mx(i):
-            o_ps = ps_a.tile([P, 2, P], F32, name="o_ps", tag="aux")
+            o_ps = ps_o.tile([P, 2, P], F32, name="o_ps", tag="o")
+            st[("o", i)] = o_ps
             for h in range(2):
                 for g in range(NG):
                     w0 = C * g + P * h
@@ -210,43 +219,43 @@ def tile_trainingfreeselfattention_kernel(tc, hidden_states, out):
                         start=(g == 0),
                         stop=(g == NG - 1),
                     )
-            nc.vector.tensor_copy(out=o_sb[:, :, P * i : P * (i + 1)], in_=o_ps[:])
-            if i % 4 == 3:
-                n0 = P * (i - 3)
+
+        def o_out(i):
+            nc.vector.tensor_copy(out=o_sb[:, :, P * i : P * (i + 1)], in_=st[("o", i)][:])
+            if i in STORE_AFTER:
+                n0 = P * (i + 1 - STORE_AFTER[i])
+                n1 = P * (i + 1)
                 b = n0 // HALF
                 for h in range(2):
                     nc.sync.dma_start(
-                        out=y[b, P * h : P * (h + 1), n0 - HALF * b : n0 - HALF * b + 512],
-                        in_=o_sb[:, h, n0 : n0 + 512],
+                        out=y[b, P * h : P * (h + 1), n0 - HALF * b : n1 - HALF * b],
+                        in_=o_sb[:, h, n0:n1],
                     )
 
         for g in range(NG):
-            score(0, g, None)
+            score(0, g, -9)
         bias(0)
 
-        for i in range(NB + 3):
+        for i in range(NB + 5):
             if 0 <= i - 1 < NB:
+                recip(i - 1)
                 for k in range(3):
                     norm(i - 1, k)
             for g in range(NG):
                 if i < NB:
                     expo(i, g)
-                weave = (i - 2, 2 * (g - 1)) if 1 <= g <= 4 else None
                 if i + 1 < NB:
-                    score(i + 1, g, weave)
-                elif weave is not None:
-                    transp(weave[0], weave[1])
-                    transp(weave[0], weave[1] + 1)
+                    score(i + 1, g, i - 2)
+                else:
+                    transp(i - 2, 2 * g)
+                    transp(i - 2, 2 * g + 1)
             if i + 1 < NB:
                 bias(i + 1)
-            evac(i - 2, 0)
-            evac(i - 2, 1)
-            for w in range(8, 12):
-                transp(i - 2, w)
-            evac(i - 2, 2)
             for k in range(3):
-                quant(i - 2, k)
-            if i < NB:
-                recip(i)
-            if 0 <= i - 3 < NB:
-                mx(i - 3)
+                evac(i - 2, k)
+            for k in range(3):
+                quant(i - 3, k)
+            if 0 <= i - 4 < NB:
+                mx(i - 4)
+            if 0 <= i - 5 < NB:
+                o_out(i - 5)

@@ -20,6 +20,8 @@ NG = NTOK // 512
 HALF = 1536
 FLOPS = 2 * 2 * NTOK * NTOK * C
 INV = 1.0 / 16.0
+SPLIT = {"a": (0, 256), "v": (256, 256), "g": (256, 3072)}
+LAST_SPLIT = {"a": (0, 896), "v": (896, 2304), "g": (2304, 3072)}
 STORE_AFTER = {3: 4, 7: 4, 11: 4, 15: 4, 19: 4, 22: 3, 23: 1}
 
 
@@ -32,7 +34,7 @@ def tile_trainingfreeselfattention_kernel(tc, hidden_states, out):
         keep = ctx.enter_context(tc.tile_pool(name="keep", bufs=1))
         small = ctx.enter_context(tc.tile_pool(name="small", bufs=4))
         big = ctx.enter_context(tc.tile_pool(name="big", bufs=4))
-        stage = ctx.enter_context(tc.tile_pool(name="stage", bufs=3))
+        stage = ctx.enter_context(tc.tile_pool(name="stage", bufs=4))
         ps_s = ctx.enter_context(tc.psum_pool(name="ps_s", bufs=3))
         ps_t = ctx.enter_context(tc.psum_pool(name="ps_t", bufs=3))
         ps_o = ctx.enter_context(tc.psum_pool(name="ps_o", bufs=2))
@@ -132,34 +134,34 @@ def tile_trainingfreeselfattention_kernel(tc, hidden_states, out):
             )
             st[("nb", i)] = nb
 
-        def expo(i, g):
-            if g == 0:
-                st[("s6", i)] = small.tile([P, NG], F32, name="s6", tag="s6")
+        def expo(i):
+            tot = small.tile([P, 1], F32, name="tot", tag="tot")
+            st[("tot", i)] = tot
             nc.scalar.activation(
-                out=st[("e", i)][:, 512 * g : 512 * (g + 1)],
-                in_=st[("e", i)][:, 512 * g : 512 * (g + 1)],
+                out=st[("e", i)][:],
+                in_=st[("e", i)][:],
                 func=AF.Exp,
                 bias=st[("nb", i)][:, 0:1],
                 scale=1.0,
-                accum_out=st[("s6", i)][:, g : g + 1],
+                accum_out=tot[:, 0:1],
             )
 
         def recip(i):
-            tot = small.tile([P, 1], F32, name="tot", tag="tot")
             r = small.tile([P, 1], F32, name="r", tag="r")
-            nc.vector.tensor_reduce(out=tot[:], in_=st[("s6", i)][:], axis=AX.X, op=ALU.add)
-            nc.vector.reciprocal(out=r[:], in_=tot[:])
+            nc.vector.reciprocal(out=r[:], in_=st[("tot", i)][:])
             st[("r", i)] = r
+            st[("a", i)] = big.tile([P, NTOK], BF16, name="a", tag="a")
 
-        def norm(i, k):
-            if k == 0:
-                st[("a", i)] = big.tile([P, NTOK], BF16, name="a", tag="a")
-            dst = st[("a", i)][:, 1024 * k : 1024 * (k + 1)]
-            src = st[("e", i)][:, 1024 * k : 1024 * (k + 1)]
+        def norm(i, eng):
+            c0, c1 = (LAST_SPLIT if i == NB - 1 else SPLIT)[eng]
+            if c0 == c1:
+                return
+            dst = st[("a", i)][:, c0:c1]
+            src = st[("e", i)][:, c0:c1]
             r = st[("r", i)][:, 0:1]
-            if i == NB - 1 and k == 0:
+            if eng == "v":
                 nc.vector.tensor_scalar(out=dst, in0=src, scalar1=r, scalar2=None, op0=ALU.mult)
-            elif i == NB - 1 and k == 1:
+            elif eng == "a":
                 nc.scalar.activation(out=dst, in_=src, func=AF.Copy, scale=r)
             else:
                 nc.gpsimd.tensor_scalar(
@@ -236,14 +238,18 @@ def tile_trainingfreeselfattention_kernel(tc, hidden_states, out):
             score(0, g, -9)
         bias(0)
 
-        for i in range(NB + 5):
+        for i in range(NB + 6):
+            for k in range(3):
+                quant(i - 4, k)
             if 0 <= i - 1 < NB:
                 recip(i - 1)
-                for k in range(3):
-                    norm(i - 1, k)
+                norm(i - 1, "g")
+                norm(i - 1, "v")
+            if i < NB:
+                expo(i)
+            if 0 <= i - 1 < NB:
+                norm(i - 1, "a")
             for g in range(NG):
-                if i < NB:
-                    expo(i, g)
                 if i + 1 < NB:
                     score(i + 1, g, i - 2)
                 else:
@@ -253,9 +259,7 @@ def tile_trainingfreeselfattention_kernel(tc, hidden_states, out):
                 bias(i + 1)
             for k in range(3):
                 evac(i - 2, k)
-            for k in range(3):
-                quant(i - 3, k)
-            if 0 <= i - 4 < NB:
-                mx(i - 4)
             if 0 <= i - 5 < NB:
-                o_out(i - 5)
+                mx(i - 5)
+            if 0 <= i - 6 < NB:
+                o_out(i - 6)

@@ -20,14 +20,14 @@ NG = NTOK // 512
 HALF = 1536
 FLOPS = 2 * 2 * NTOK * NTOK * C
 INV = 1.0 / 16.0
-SPLIT = {"a": (0, 256), "v": (256, 256), "g": (256, 3072)}
-LAST_SPLIT = {"a": (0, 896), "v": (896, 2304), "g": (2304, 3072)}
-STORE_AFTER = {3: 4, 7: 4, 11: 4, 15: 4, 19: 4, 22: 3, 23: 1}
+XA = 256
+WARM = 5
+STORE_AFTER = {3: 4, 7: 4, 11: 4, 15: 4, 19: 4, 22: 3}
 
 
 def tile_trainingfreeselfattention_kernel(tc, hidden_states, out):
     nc = tc.nc
-    x = hidden_states.rearrange("b c h w -> b c (h w)")
+    x = hidden_states.rearrange("b (h p) y x -> b p h (y x)", p=P)
     y = out.rearrange("b c h w -> b c (h w)")
 
     with ExitStack() as ctx:
@@ -41,36 +41,25 @@ def tile_trainingfreeselfattention_kernel(tc, hidden_states, out):
         ctx.enter_context(tc.manual_schedule())
 
         f_t = keep.tile([P, 2, NTOK], BF16, name="f_t")
-        f_p = keep.tile([P, 2, NTOK], BF16, name="f_p")
         ident = keep.tile([P, P], F32, name="ident")
+        zeros = keep.tile([P, 512], BF16, name="zeros")
         f_codes = keep.tile([P, NG * C], U32, name="f_codes", align_bytes=64)
         f_scales = keep.tile([P, NG * C], U8, name="f_scales", align_bytes=64)
         o_sb = keep.tile([P, 2, NTOK], F32, name="o_sb")
         warm_in = keep.tile([P, 1], F32, name="warm_in")
         warm_out = keep.tile([P, 1], F32, name="warm_out")
 
-        for b in range(2):
-            for h in range(2):
-                nc.sync.dma_start(
-                    out=f_t[:, h, HALF * b : HALF * (b + 1)],
-                    in_=x[b, P * h : P * (h + 1), :],
-                )
+        for g in range(NG):
+            b = (512 * g) // HALF
+            c0 = 512 * g - HALF * b
+            nc.sync.dma_start(out=f_t[:, :, 512 * g : 512 * (g + 1)], in_=x[b, :, :, c0 : c0 + 512])
+        nc.vector.memset(zeros[:], 0.0)
         nc.vector.memset(warm_in[:], 0.0)
         nc.scalar.activation(out=warm_out[:], in_=warm_in[:], func=AF.Exp)
         make_identity(nc, ident[:])
-
-        for g in range(NG):
-            for h in range(2):
-                src = f_t[:, h, 512 * g : 512 * (g + 1)].bitcast(F32).rearrange(
-                    "p (q u) -> p u q", u=2
-                )
-                dst = f_p[:, h, 512 * g : 512 * (g + 1)].bitcast(F32).rearrange(
-                    "p (u q) -> p u q", u=2
-                )
-                if h == 0:
-                    nc.vector.tensor_copy(out=dst, in_=src)
-                else:
-                    nc.scalar.copy(out=dst, in_=src)
+        dummy = ps_s.tile([P, 512], F32, name="dummy", tag="s")
+        for w in range(WARM):
+            nc.tensor.matmul(dummy[:], lhsT=zeros[:, 0:P], rhs=zeros[:], start=True, stop=True)
 
         st = {}
 
@@ -86,7 +75,7 @@ def tile_trainingfreeselfattention_kernel(tc, hidden_states, out):
                 c0 = 256 * g + P * u
                 nc.tensor.transpose(
                     st[("t", i, w // 4)][:, u, P * h : P * (h + 1)],
-                    f_p[:, h, :].bitcast(F32)[:, c0 : c0 + P],
+                    f_t[:, h, :].bitcast(F32)[:, c0 : c0 + P],
                     ident[:],
                 )
                 return
@@ -98,6 +87,10 @@ def tile_trainingfreeselfattention_kernel(tc, hidden_states, out):
                 ident[:],
             )
 
+        def transp_all(i):
+            for w in range(12):
+                transp(i, w)
+
         def score(i, g, j):
             if g == 0:
                 st[("e", i)] = big.tile([P, NTOK], F32, name="e", tag="e")
@@ -107,7 +100,7 @@ def tile_trainingfreeselfattention_kernel(tc, hidden_states, out):
                 nc.tensor.matmul(
                     s[:],
                     lhsT=f_t[:, h, P * i : P * (i + 1)],
-                    rhs=f_p[:, h, 512 * g : 512 * (g + 1)],
+                    rhs=f_t[:, h, 512 * g : 512 * (g + 1)],
                     start=(h == 0),
                     stop=(h == 1),
                 )
@@ -152,10 +145,7 @@ def tile_trainingfreeselfattention_kernel(tc, hidden_states, out):
             st[("r", i)] = r
             st[("a", i)] = big.tile([P, NTOK], BF16, name="a", tag="a")
 
-        def norm(i, eng):
-            c0, c1 = (LAST_SPLIT if i == NB - 1 else SPLIT)[eng]
-            if c0 == c1:
-                return
+        def norm(i, eng, c0, c1):
             dst = st[("a", i)][:, c0:c1]
             src = st[("e", i)][:, c0:c1]
             r = st[("r", i)][:, 0:1]
@@ -168,42 +158,59 @@ def tile_trainingfreeselfattention_kernel(tc, hidden_states, out):
                     out=dst, in0=src, scalar1=r, scalar2=0.0, op0=ALU.mult, op1=ALU.add
                 )
 
-        def evac(i, k):
+        def evac(i, k, eng):
             if not -2 <= i < NB:
                 return
             if k == 0:
                 st[("g4", i)] = stage.tile([P, NTOK], BF16, name="g4", tag="g4", align_bytes=64)
             dst32 = st[("g4", i)][:].bitcast(F32)[:, 512 * k : 512 * (k + 1)]
             if i < 0:
-                nc.scalar.copy(
-                    out=dst32.rearrange("p (c u) -> p c u", u=2),
-                    in_=st[("t", i, k)][:].rearrange("p u c -> p c u"),
-                )
+                dst = dst32.rearrange("p (c u) -> p c u", u=2)
+                src = st[("t", i, k)][:].rearrange("p u c -> p c u")
             else:
-                nc.scalar.copy(
-                    out=dst32.rearrange("p (g n u) -> p g n u", g=2, u=2),
-                    in_=st[("t", i, k)][:].rearrange("p g u n -> p g n u"),
-                )
+                dst = dst32.rearrange("p (g n u) -> p g n u", g=2, u=2)
+                src = st[("t", i, k)][:].rearrange("p g u n -> p g n u")
+            if eng == "v":
+                nc.vector.tensor_copy(out=dst, in_=src)
+            else:
+                nc.scalar.copy(out=dst, in_=src)
 
-        def quant(i, k):
+        def evac_all(i, eng):
+            for k in range(3):
+                evac(i, k, eng)
+
+        def quant(i):
             if not -2 <= i < NB:
                 return
-            src = st[("g4", i)][:, 1024 * k : 1024 * (k + 1)]
-            if i < 0:
-                g = 3 * (i + 2) + k
-                nc.vector.quantize_mx(
-                    out=f_codes[:, C * g : C * (g + 1)].bitcast(FP8X4),
-                    scales=f_scales[:, C * g : C * (g + 1)],
-                    in_=src,
-                )
-                return
-            if k == 0:
+            if i >= 0:
                 st[("qc", i)] = stage.tile([P, NG * P], U32, name="qc", tag="qc", align_bytes=64)
                 st[("qs", i)] = stage.tile([P, NG * P], U8, name="qs", tag="qs", align_bytes=64)
-            nc.vector.quantize_mx(
-                out=st[("qc", i)][:, 256 * k : 256 * (k + 1)].bitcast(FP8X4),
-                scales=st[("qs", i)][:, 256 * k : 256 * (k + 1)],
-                in_=src,
+            for k in range(3):
+                src = st[("g4", i)][:, 1024 * k : 1024 * (k + 1)]
+                if i < 0:
+                    g = 3 * (i + 2) + k
+                    nc.vector.quantize_mx(
+                        out=f_codes[:, C * g : C * (g + 1)].bitcast(FP8X4),
+                        scales=f_scales[:, C * g : C * (g + 1)],
+                        in_=src,
+                    )
+                else:
+                    nc.vector.quantize_mx(
+                        out=st[("qc", i)][:, 256 * k : 256 * (k + 1)].bitcast(FP8X4),
+                        scales=st[("qs", i)][:, 256 * k : 256 * (k + 1)],
+                        in_=src,
+                    )
+
+        def mx_pass(i, dst, h, g):
+            w0 = C * g + P * h
+            nc.tensor.matmul_mx(
+                out=dst,
+                lhsT=f_codes[:, w0 : w0 + P].bitcast(FP8X4),
+                lhsT_scale=f_scales[:, w0 : w0 + P],
+                rhs=st[("qc", i)][:, P * g : P * (g + 1)].bitcast(FP8X4),
+                rhs_scale=st[("qs", i)][:, P * g : P * (g + 1)],
+                start=(g == 0),
+                stop=(g == NG - 1),
             )
 
         def mx(i):
@@ -211,19 +218,9 @@ def tile_trainingfreeselfattention_kernel(tc, hidden_states, out):
             st[("o", i)] = o_ps
             for h in range(2):
                 for g in range(NG):
-                    w0 = C * g + P * h
-                    nc.tensor.matmul_mx(
-                        out=o_ps[:, h, :],
-                        lhsT=f_codes[:, w0 : w0 + P].bitcast(FP8X4),
-                        lhsT_scale=f_scales[:, w0 : w0 + P],
-                        rhs=st[("qc", i)][:, P * g : P * (g + 1)].bitcast(FP8X4),
-                        rhs_scale=st[("qs", i)][:, P * g : P * (g + 1)],
-                        start=(g == 0),
-                        stop=(g == NG - 1),
-                    )
+                    mx_pass(i, o_ps[:, h, :], h, g)
 
-        def o_out(i):
-            nc.vector.tensor_copy(out=o_sb[:, :, P * i : P * (i + 1)], in_=st[("o", i)][:])
+        def store(i):
             if i in STORE_AFTER:
                 n0 = P * (i + 1 - STORE_AFTER[i])
                 n1 = P * (i + 1)
@@ -234,32 +231,69 @@ def tile_trainingfreeselfattention_kernel(tc, hidden_states, out):
                         in_=o_sb[:, h, n0:n1],
                     )
 
+        def o_out(i, eng):
+            dst = o_sb[:, :, P * i : P * (i + 1)]
+            if eng == "v":
+                nc.vector.tensor_copy(out=dst, in_=st[("o", i)][:])
+            else:
+                nc.scalar.copy(out=dst, in_=st[("o", i)][:])
+            store(i)
+
         for g in range(NG):
             score(0, g, -9)
         bias(0)
 
-        for i in range(NB + 6):
-            for k in range(3):
-                quant(i - 4, k)
-            if 0 <= i - 1 < NB:
+        for i in range(NB - 1):
+            quant(i - 4)
+            if i >= 1:
                 recip(i - 1)
-                norm(i - 1, "g")
-                norm(i - 1, "v")
-            if i < NB:
-                expo(i)
-            if 0 <= i - 1 < NB:
-                norm(i - 1, "a")
+                norm(i - 1, "g", XA, NTOK)
+            expo(i)
+            if i >= 1:
+                norm(i - 1, "a", 0, XA)
             for g in range(NG):
-                if i + 1 < NB:
-                    score(i + 1, g, i - 2)
-                else:
-                    transp(i - 2, 2 * g)
-                    transp(i - 2, 2 * g + 1)
-            if i + 1 < NB:
-                bias(i + 1)
-            for k in range(3):
-                evac(i - 2, k)
-            if 0 <= i - 5 < NB:
+                score(i + 1, g, i - 2)
+            bias(i + 1)
+            evac_all(i - 2, "a")
+            if i >= 5:
                 mx(i - 5)
-            if 0 <= i - 6 < NB:
-                o_out(i - 6)
+            if i >= 6:
+                o_out(i - 6, "v")
+
+        last = NB - 1
+        expo(last)
+        transp_all(last - 2)
+        recip(last - 1)
+        norm(last - 1, "g", HALF, NTOK)
+        evac_all(last - 2, "v")
+        mx(last - 5)
+        norm(last - 1, "v", 0, HALF)
+        transp_all(last - 1)
+        quant(last - 4)
+        o_out(last - 6, "v")
+        mx(last - 4)
+        evac_all(last - 1, "a")
+        recip(last)
+        norm(last, "v", 0, NTOK)
+        transp_all(last)
+        quant(last - 3)
+        o_out(last - 5, "a")
+        mx(last - 3)
+        evac_all(last, "a")
+        quant(last - 2)
+        o_out(last - 4, "a")
+        mx(last - 2)
+        quant(last - 1)
+        o_out(last - 3, "a")
+        mx(last - 1)
+        o_out(last - 2, "a")
+        quant(last)
+        o_h = [ps_s.tile([P, 512], F32, name="o_h", tag="s") for h in range(2)]
+        for g in range(NG):
+            for h in range(2):
+                mx_pass(last, o_h[h][:, 0:P], h, g)
+        o_out(last - 1, "a")
+        nc.vector.tensor_copy(out=o_sb[:, 0, P * last : NTOK], in_=o_h[0][:, 0:P])
+        nc.scalar.copy(out=o_sb[:, 1, P * last : NTOK], in_=o_h[1][:, 0:P])
+        nc.sync.dma_start(out=y[1, 0:P, HALF - P : HALF], in_=o_sb[:, 0, P * last : NTOK])
+        nc.sync.dma_start(out=y[1, P:C, HALF - P : HALF], in_=o_sb[:, 1, P * last : NTOK])

@@ -20,7 +20,7 @@ NG = NTOK // 512
 HALF = 1536
 FLOPS = 2 * 2 * NTOK * NTOK * C
 INV = 1.0 / 16.0
-XA = 256
+XA = 160
 WARM = 5
 STORE_AFTER = {3: 4, 7: 4, 11: 4, 15: 4, 19: 4, 22: 3}
 
@@ -254,7 +254,9 @@ def tile_trainingfreeselfattention_kernel(tc, hidden_states, out):
             for g in range(NG):
                 score(i + 1, g, i - 2)
             bias(i + 1)
-            evac_all(i - 2, "a")
+            evac(i - 2, 0, "a")
+            evac(i - 2, 1, "a")
+            evac(i - 2, 2, "v" if i < 2 else "a")
             if i >= 5:
                 mx(i - 5)
             if i >= 6:

from contextlib import ExitStack

import concourse.mybir as mybir
from concourse.masks import make_identity

F32 = mybir.dt.float32
BF16 = mybir.dt.bfloat16
U32 = mybir.dt.uint32
U8 = mybir.dt.uint8
FP8X4 = mybir.dt.float8_e4m3fn_x4
AF = mybir.ActivationFunctionType
ALU = mybir.AluOpType
AX = mybir.AxisListType

P = 128
C = 256
NTOK = 3072
NB = NTOK // P
NG = NTOK // 512
HALF = 1536
FLOPS = 2 * 2 * NTOK * NTOK * C
INV = 1.0 / 16.0
XA = 160
WARM = 5
STORE_AFTER = {3: 4, 7: 4, 11: 4, 15: 4, 19: 4, 22: 3}


def tile_trainingfreeselfattention_kernel(tc, hidden_states, out):
    nc = tc.nc
    x = hidden_states.rearrange("b (h p) y x -> b p h (y x)", p=P)
    y = out.rearrange("b c h w -> b c (h w)")

    with ExitStack() as ctx:
        keep = ctx.enter_context(tc.tile_pool(name="keep", bufs=1))
        small = ctx.enter_context(tc.tile_pool(name="small", bufs=4))
        big = ctx.enter_context(tc.tile_pool(name="big", bufs=4))
        stage = ctx.enter_context(tc.tile_pool(name="stage", bufs=4))
        ps_s = ctx.enter_context(tc.psum_pool(name="ps_s", bufs=3))
        ps_t = ctx.enter_context(tc.psum_pool(name="ps_t", bufs=3))
        ps_o = ctx.enter_context(tc.psum_pool(name="ps_o", bufs=2))
        ctx.enter_context(tc.manual_schedule())

        f_t = keep.tile([P, 2, NTOK], BF16, name="f_t")
        ident = keep.tile([P, P], F32, name="ident")
        zeros = keep.tile([P, 512], BF16, name="zeros")
        f_codes = keep.tile([P, NG * C], U32, name="f_codes", align_bytes=64)
        f_scales = keep.tile([P, NG * C], U8, name="f_scales", align_bytes=64)
        o_sb = keep.tile([P, 2, NTOK], F32, name="o_sb")
        warm_in = keep.tile([P, 1], F32, name="warm_in")
        warm_out = keep.tile([P, 1], F32, name="warm_out")

        for g in range(NG):
            b = (512 * g) // HALF
            c0 = 512 * g - HALF * b
            nc.sync.dma_start(out=f_t[:, :, 512 * g : 512 * (g + 1)], in_=x[b, :, :, c0 : c0 + 512])
        nc.vector.memset(zeros[:], 0.0)
        nc.vector.memset(warm_in[:], 0.0)
        nc.scalar.activation(out=warm_out[:], in_=warm_in[:], func=AF.Exp)
        make_identity(nc, ident[:])
        dummy = ps_s.tile([P, 512], F32, name="dummy", tag="s")
        for w in range(WARM):
            nc.tensor.matmul(dummy[:], lhsT=zeros[:, 0:P], rhs=zeros[:], start=True, stop=True)

        st = {}

        def transp(i, w):
            if not -2 <= i < NB:
                return
            if i < 0:
                g = 3 * (i + 2) + w // 4
                if w % 4 == 0:
                    st[("t", i, w // 4)] = ps_t.tile([P, 2, C], F32, name="tf", tag="t")
                u = (w // 2) % 2
                h = w % 2
                c0 = 256 * g + P * u
                nc.tensor.transpose(
                    st[("t", i, w // 4)][:, u, P * h : P * (h + 1)],
                    f_t[:, h, :].bitcast(F32)[:, c0 : c0 + P],
                    ident[:],
                )
                return
            if w % 4 == 0:
                st[("t", i, w // 4)] = ps_t.tile([P, 2, 2, P], F32, name="t", tag="t")
            nc.tensor.transpose(
                st[("t", i, w // 4)][:, (w // 2) % 2, w % 2, :],
                st[("a", i)][:].bitcast(F32)[:, P * w : P * (w + 1)],
                ident[:],
            )

        def transp_all(i):
            for w in range(12):
                transp(i, w)

        def score(i, g, j):
            if g == 0:
                st[("e", i)] = big.tile([P, NTOK], F32, name="e", tag="e")
                st[("m6", i)] = small.tile([P, NG], F32, name="m6", tag="m6")
            s = ps_s.tile([P, 512], F32, name="s", tag="s")
            for h in range(2):
                nc.tensor.matmul(
                    s[:],
                    lhsT=f_t[:, h, P * i : P * (i + 1)],
                    rhs=f_t[:, h, 512 * g : 512 * (g + 1)],
                    start=(h == 0),
                    stop=(h == 1),
                )
                m = 2 * g + h
                if m < 10:
                    transp(j, m)
                elif m == 10:
                    transp(j, 10)
                    transp(j, 11)
            nc.vector.tensor_scalar(
                out=st[("e", i)][:, 512 * g : 512 * (g + 1)],
                in0=s[:],
                scalar1=INV,
                scalar2=None,
                op0=ALU.mult,
                op1=ALU.max,
                accum_out=st[("m6", i)][:, g : g + 1],
            )

        def bias(i):
            nb = small.tile([P, 1], F32, name="nb", tag="nb")
            nc.vector.tensor_reduce(
                out=nb[:], in_=st[("m6", i)][:], axis=AX.X, op=ALU.max, negate=True
            )
            st[("nb", i)] = nb

        def expo(i):
            tot = small.tile([P, 1], F32, name="tot", tag="tot")
            st[("tot", i)] = tot
            nc.scalar.activation(
                out=st[("e", i)][:],
                in_=st[("e", i)][:],
                func=AF.Exp,
                bias=st[("nb", i)][:, 0:1],
                scale=1.0,
                accum_out=tot[:, 0:1],
            )

        def recip(i):
            r = small.tile([P, 1], F32, name="r", tag="r")
            nc.vector.reciprocal(out=r[:], in_=st[("tot", i)][:])
            st[("r", i)] = r
            st[("a", i)] = big.tile([P, NTOK], BF16, name="a", tag="a")

        def norm(i, eng, c0, c1):
            dst = st[("a", i)][:, c0:c1]
            src = st[("e", i)][:, c0:c1]
            r = st[("r", i)][:, 0:1]
            if eng == "v":
                nc.vector.tensor_scalar(out=dst, in0=src, scalar1=r, scalar2=None, op0=ALU.mult)
            elif eng == "a":
                nc.scalar.activation(out=dst, in_=src, func=AF.Copy, scale=r)
            else:
                nc.gpsimd.tensor_scalar(
                    out=dst, in0=src, scalar1=r, scalar2=0.0, op0=ALU.mult, op1=ALU.add
                )

        def evac(i, k, eng):
            if not -2 <= i < NB:
                return
            if k == 0:
                st[("g4", i)] = stage.tile([P, NTOK], BF16, name="g4", tag="g4", align_bytes=64)
            dst32 = st[("g4", i)][:].bitcast(F32)[:, 512 * k : 512 * (k + 1)]
            if i < 0:
                dst = dst32.rearrange("p (c u) -> p c u", u=2)
                src = st[("t", i, k)][:].rearrange("p u c -> p c u")
            else:
                dst = dst32.rearrange("p (g n u) -> p g n u", g=2, u=2)
                src = st[("t", i, k)][:].rearrange("p g u n -> p g n u")
            if eng == "v":
                nc.vector.tensor_copy(out=dst, in_=src)
            else:
                nc.scalar.copy(out=dst, in_=src)

        def evac_all(i, eng):
            for k in range(3):
                evac(i, k, eng)

        def quant(i):
            if not -2 <= i < NB:
                return
            if i >= 0:
                st[("qc", i)] = stage.tile([P, NG * P], U32, name="qc", tag="qc", align_bytes=64)
                st[("qs", i)] = stage.tile([P, NG * P], U8, name="qs", tag="qs", align_bytes=64)
            for k in range(3):
                src = st[("g4", i)][:, 1024 * k : 1024 * (k + 1)]
                if i < 0:
                    g = 3 * (i + 2) + k
                    nc.vector.quantize_mx(
                        out=f_codes[:, C * g : C * (g + 1)].bitcast(FP8X4),
                        scales=f_scales[:, C * g : C * (g + 1)],
                        in_=src,
                    )
                else:
                    nc.vector.quantize_mx(
                        out=st[("qc", i)][:, 256 * k : 256 * (k + 1)].bitcast(FP8X4),
                        scales=st[("qs", i)][:, 256 * k : 256 * (k + 1)],
                        in_=src,
                    )

        def mx_pass(i, dst, h, g):
            w0 = C * g + P * h
            nc.tensor.matmul_mx(
                out=dst,
                lhsT=f_codes[:, w0 : w0 + P].bitcast(FP8X4),
                lhsT_scale=f_scales[:, w0 : w0 + P],
                rhs=st[("qc", i)][:, P * g : P * (g + 1)].bitcast(FP8X4),
                rhs_scale=st[("qs", i)][:, P * g : P * (g + 1)],
                start=(g == 0),
                stop=(g == NG - 1),
            )

        def mx(i):
            o_ps = ps_o.tile([P, 2, P], F32, name="o_ps", tag="o")
            st[("o", i)] = o_ps
            for h in range(2):
                for g in range(NG):
                    mx_pass(i, o_ps[:, h, :], h, g)

        def store(i):
            if i in STORE_AFTER:
                n0 = P * (i + 1 - STORE_AFTER[i])
                n1 = P * (i + 1)
                b = n0 // HALF
                for h in range(2):
                    nc.sync.dma_start(
                        out=y[b, P * h : P * (h + 1), n0 - HALF * b : n1 - HALF * b],
                        in_=o_sb[:, h, n0:n1],
                    )

        def o_out(i, eng):
            dst = o_sb[:, :, P * i : P * (i + 1)]
            if eng == "v":
                nc.vector.tensor_copy(out=dst, in_=st[("o", i)][:])
            else:
                nc.scalar.copy(out=dst, in_=st[("o", i)][:])
            store(i)

        for g in range(NG):
            score(0, g, -9)
        bias(0)

        for i in range(NB - 1):
            quant(i - 4)
            if i >= 1:
                recip(i - 1)
                norm(i - 1, "g", XA, NTOK)
            expo(i)
            if i >= 1:
                norm(i - 1, "a", 0, XA)
            for g in range(NG):
                score(i + 1, g, i - 2)
            bias(i + 1)
            evac(i - 2, 0, "a")
            evac(i - 2, 1, "a")
            evac(i - 2, 2, "v" if i < 2 else "a")
            if i >= 5:
                mx(i - 5)
            if i >= 6:
                o_out(i - 6, "v")

        last = NB - 1
        expo(last)
        transp_all(last - 2)
        recip(last - 1)
        norm(last - 1, "g", HALF, NTOK)
        evac_all(last - 2, "v")
        mx(last - 5)
        norm(last - 1, "v", 0, HALF)
        transp_all(last - 1)
        quant(last - 4)
        o_out(last - 6, "v")
        mx(last - 4)
        evac_all(last - 1, "a")
        recip(last)
        norm(last, "v", 0, NTOK)
        transp_all(last)
        quant(last - 3)
        o_out(last - 5, "a")
        mx(last - 3)
        evac_all(last, "a")
        quant(last - 2)
        o_out(last - 4, "a")
        mx(last - 2)
        quant(last - 1)
        o_out(last - 3, "a")
        mx(last - 1)
        o_out(last - 2, "a")
        quant(last)
        o_h = [ps_s.tile([P, 512], F32, name="o_h", tag="s") for h in range(2)]
        for g in range(NG):
            for h in range(2):
                mx_pass(last, o_h[h][:, 0:P], h, g)
        o_out(last - 1, "a")
        nc.vector.tensor_copy(out=o_sb[:, 0, P * last : NTOK], in_=o_h[0][:, 0:P])
        nc.scalar.copy(out=o_sb[:, 1, P * last : NTOK], in_=o_h[1][:, 0:P])
        nc.sync.dma_start(out=y[1, 0:P, HALF - P : HALF], in_=o_sb[:, 0, P * last : NTOK])
        nc.sync.dma_start(out=y[1, P:C, HALF - P : HALF], in_=o_sb[:, 1, P * last : NTOK])
